import numpy as np
import ml_dtypes

BF16 = ml_dtypes.bfloat16


def bf(x):
    return np.asarray(x, np.float32).astype(BF16)


def f32(x):
    return np.asarray(x, np.float32)


def f64(x):
    return np.asarray(x).astype(np.float64)


def striped(idx):
    return np.tile(idx.reshape(-1, 16).T, (8, 1))


V, E, H, M, N = 2048, 128, 128, 512, 1024


def sigmoid(v):
    return 1.0 / (1.0 + np.exp(-v))


def setup_inputs():
    return {"table": bf(np.random.standard_normal((V, E))), "w_ih": bf(np.random.standard_normal((E, M)) / np.sqrt(E)), "w_hh": bf(np.random.standard_normal((H, M)) / np.sqrt(H)), "h0": bf(np.random.standard_normal((H, N))), "c0": f32(np.random.standard_normal((H, N))), "b_ih": f32(0.1 * np.random.standard_normal((M, 1))), "b_hh": f32(0.1 * np.random.standard_normal((M, 1))), "offs": striped(np.random.permutation(np.tile(np.arange(V), 2))[:N])}


def reference(table, w_ih, w_hh, h0, c0, b_ih, b_hh, offs):
    idx = offs[:16].T.reshape(-1)
    z = f64(w_ih).T @ f64(table)[idx].T + f64(w_hh).T @ f64(h0) + f64(b_ih) + f64(b_hh)
    z_in, z_forget, z_cell, z_out = z.reshape(M // H, H, N)
    c = sigmoid(z_forget) * f64(c0) + sigmoid(z_in) * np.tanh(z_cell)
    return sigmoid(z_out) * np.tanh(c)

@@ -1,0 +1,133 @@
+import concourse.masks as masks
+import concourse.mybir as mybir
+
+BF16, F32, U16 = mybir.dt.bfloat16, mybir.dt.float32, mybir.dt.uint16
+SIGMOID = mybir.ActivationFunctionType.Sigmoid
+TANH = mybir.ActivationFunctionType.Tanh
+
+P = 128
+V, E, H, N = 2048, 128, 128, 1024
+IN_GATE, FORGET_GATE, CELL_GATE, OUT_GATE = 0, 1, 2, 3
+GATES = 4
+CELL_STATE_GATES = (FORGET_GATE, IN_GATE, CELL_GATE)
+PIECE = 512
+PIECES = N // PIECE
+CHUNK = 512
+CHUNKS = V // CHUNK
+BLOCKS = CHUNK // P
+BANKS = 8
+
+FLOPS = 2 * GATES * H * N * (E + H)
+BYTES = 2 * N * E + 2 * GATES * H * (E + H) + 2 * H * N + 4 * H * N + 2 * 4 * GATES * H + 2 * P * (N // 16) + 4 * H * N
+
+
+def tile_attnseqdecoder_kernel(tc, table, w_ih, w_hh, h0, c0, b_ih, b_hh, offs, out):
+    nc = tc.nc
+    with (
+        tc.tile_pool(name="held", bufs=1) as held,
+        tc.tile_pool(name="stage", bufs=CHUNKS) as stage,
+        tc.tile_pool(name="work", bufs=PIECES) as work,
+        tc.psum_pool(name="psum", bufs=BANKS) as psum,
+    ):
+        b_ih_rows = held.tile([GATES, H], F32, name="b_ih_rows")
+        nc.sync.dma_start(b_ih_rows[:], b_ih.rearrange("(g r) o -> g (r o)", g=GATES))
+        b_hh_rows = held.tile([GATES, H], F32, name="b_hh_rows")
+        nc.sync.dma_start(b_hh_rows[:], b_hh.rearrange("(g r) o -> g (r o)", g=GATES))
+        w_hh_sb = held.tile([H, GATES * H], BF16, name="w_hh_sb")
+        nc.sync.dma_start(w_hh_sb[:], w_hh)
+        h0_sb = held.tile([H, N], BF16, name="h0_sb")
+        nc.scalar.dma_start(h0_sb[:], h0)
+
+        table_blocks = table.rearrange("(b p) e -> p b e", p=P)
+        rows = []
+        for chunk in range(CHUNKS):
+            rows.append(stage.tile([P, BLOCKS, E], BF16, name="rows"))
+            queue = nc.sync if chunk % 2 == 0 else nc.scalar
+            queue.dma_start(rows[chunk][:], table_blocks[:, chunk * BLOCKS : (chunk + 1) * BLOCKS, :])
+
+        offsets = held.tile([P, N // 16], U16, name="offsets")
+        nc.sync.dma_start(offsets[:], offs)
+        w_ih_sb = held.tile([E, GATES * H], BF16, name="w_ih_sb")
+        nc.sync.dma_start(w_ih_sb[:], w_ih)
+        c0_sb = held.tile([H, N], F32, name="c0_sb")
+        nc.scalar.dma_start(c0_sb[:], c0)
+
+        small_identity = held.tile([GATES, GATES], F32, name="small_identity")
+        masks.make_identity(nc, small_identity[:])
+        bias_ps = psum.tile([H, GATES], F32, name="bias_ps", tag="bank")
+        nc.tensor.matmul(bias_ps[:], b_ih_rows[:], small_identity[:], start=True, stop=False)
+        nc.tensor.matmul(bias_ps[:], b_hh_rows[:], small_identity[:], start=False, stop=True)
+        bias = held.tile([H, GATES], F32, name="bias")
+        nc.vector.tensor_copy(bias[:], bias_ps[:])
+
+        z = {}
+
+        def hidden_part(gate, piece):
+            z[gate, piece] = psum.tile([H, PIECE], F32, name="z", tag="bank")
+            nc.tensor.matmul(
+                z[gate, piece][:],
+                w_hh_sb[:, gate * H : (gate + 1) * H],
+                h0_sb[:, piece * PIECE : (piece + 1) * PIECE],
+                start=True,
+                stop=False,
+            )
+
+        def embedding_part(gate, piece):
+            nc.tensor.matmul(
+                z[gate, piece][:],
+                w_ih_sb[:, gate * H : (gate + 1) * H],
+                words[:].indirect(offsets[:, piece * (PIECE // 16) : (piece + 1) * (PIECE // 16)]),
+                start=False,
+                stop=True,
+            )
+
+        for gate in CELL_STATE_GATES:
+            hidden_part(gate, 0)
+
+        identity = held.tile([P, P], BF16, name="identity")
+        masks.make_identity(nc, identity[:])
+        words = held.tile([E, V], BF16, name="words")
+        for chunk in range(CHUNKS):
+            flipped = psum.tile([E, CHUNK], BF16, name="flipped", tag="bank")
+            for block in range(BLOCKS):
+                nc.tensor.transpose(flipped[:, block * P : (block + 1) * P], rows[chunk][:, block, :], identity[:])
+            if chunk % 2 == 0:
+                nc.vector.tensor_copy(words[:, chunk * CHUNK : (chunk + 1) * CHUNK], flipped[:])
+            else:
+                nc.scalar.copy(words[:, chunk * CHUNK : (chunk + 1) * CHUNK], flipped[:])
+
+        for gate in CELL_STATE_GATES:
+            hidden_part(gate, 1)
+        for piece in range(PIECES):
+            hidden_part(OUT_GATE, piece)
+
+        for piece in range(PIECES):
+            for gate in CELL_STATE_GATES:
+                embedding_part(gate, piece)
+        for piece in range(PIECES):
+            embedding_part(OUT_GATE, piece)
+
+        def gate_value(gate, piece, func, name):
+            value = work.tile([H, PIECE], F32, name=name)
+            nc.scalar.activation(value[:], z[gate, piece][:], func, bias=bias[:, gate : gate + 1])
+            return value
+
+        cell = {}
+        for piece in range(PIECES):
+            forget = gate_value(FORGET_GATE, piece, SIGMOID, "forget")
+            kept = work.tile([H, PIECE], F32, name="kept")
+            nc.vector.tensor_mul(kept[:], forget[:], c0_sb[:, piece * PIECE : (piece + 1) * PIECE])
+            let_in = gate_value(IN_GATE, piece, SIGMOID, "let_in")
+            candidate = gate_value(CELL_GATE, piece, TANH, "candidate")
+            fresh = work.tile([H, PIECE], F32, name="fresh")
+            nc.vector.tensor_mul(fresh[:], let_in[:], candidate[:])
+            cell[piece] = work.tile([H, PIECE], F32, name="cell")
+            nc.vector.tensor_add(cell[piece][:], kept[:], fresh[:])
+
+        for piece in range(PIECES):
+            let_out = gate_value(OUT_GATE, piece, SIGMOID, "let_out")
+            squashed = work.tile([H, PIECE], F32, name="squashed")
+            nc.scalar.activation(squashed[:], cell[piece][:], TANH)
+            hidden = work.tile([H, PIECE], F32, name="hidden")
+            nc.vector.tensor_mul(hidden[:], let_out[:], squashed[:])
+            nc.sync.dma_start(out[:, piece * PIECE : (piece + 1) * PIECE], hidden[:])

@@ -15,6 +15,7 @@ PIECES = N // PIECE
 CHUNK = 512
 CHUNKS = V // CHUNK
 BLOCKS = CHUNK // P
+WARM_UP = 4
 BANKS = 8
 
 FLOPS = 2 * GATES * H * N * (E + H)
@@ -51,6 +52,12 @@ def tile_attnseqdecoder_kernel(tc, table, w_ih, w_hh, h0, c0, b_ih, b_hh, offs, 
         nc.sync.dma_start(w_ih_sb[:], w_ih)
         c0_sb = held.tile([H, N], F32, name="c0_sb")
         nc.scalar.dma_start(c0_sb[:], c0)
+
+        zeros = held.tile([P, PIECE], BF16, name="zeros")
+        nc.vector.memset(zeros[:], 0.0)
+        unread = psum.tile([P, PIECE], F32, name="unread", tag="bank")
+        for repeat in range(WARM_UP):
+            nc.tensor.matmul(unread[:], zeros[:, 0:P], zeros[:], start=True, stop=True)
 
         small_identity = held.tile([GATES, GATES], F32, name="small_identity")
         masks.make_identity(nc, small_identity[:])

@@ -15,7 +15,6 @@ PIECES = N // PIECE
 CHUNK = 512
 CHUNKS = V // CHUNK
 BLOCKS = CHUNK // P
-WARM_UP = 4
 BANKS = 8
 
 FLOPS = 2 * GATES * H * N * (E + H)
@@ -53,11 +52,10 @@ def tile_attnseqdecoder_kernel(tc, table, w_ih, w_hh, h0, c0, b_ih, b_hh, offs, 
         c0_sb = held.tile([H, N], F32, name="c0_sb")
         nc.scalar.dma_start(c0_sb[:], c0)
 
-        zeros = held.tile([P, PIECE], BF16, name="zeros")
-        nc.vector.memset(zeros[:], 0.0)
-        unread = psum.tile([P, PIECE], F32, name="unread", tag="bank")
-        for repeat in range(WARM_UP):
-            nc.tensor.matmul(unread[:], zeros[:, 0:P], zeros[:], start=True, stop=True)
+        nothing = held.tile([P, 1], F32, name="nothing")
+        nc.vector.memset(nothing[:], 0.0)
+        half = held.tile([P, 1], F32, name="half")
+        nc.scalar.activation(half[:], nothing[:], SIGMOID)
 
         small_identity = held.tile([GATES, GATES], F32, name="small_identity")
         masks.make_identity(nc, small_identity[:])

@@ -12,9 +12,11 @@ GATES = 4
 CELL_STATE_GATES = (FORGET_GATE, IN_GATE, CELL_GATE)
 PIECE = 512
 PIECES = N // PIECE
+HALF = PIECE // 2
 CHUNK = 512
 CHUNKS = V // CHUNK
 BLOCKS = CHUNK // P
+WARM_UP = 4
 BANKS = 8
 
 FLOPS = 2 * GATES * H * N * (E + H)
@@ -35,8 +37,8 @@ def tile_attnseqdecoder_kernel(tc, table, w_ih, w_hh, h0, c0, b_ih, b_hh, offs, 
         nc.sync.dma_start(b_hh_rows[:], b_hh.rearrange("(g r) o -> g (r o)", g=GATES))
         w_hh_sb = held.tile([H, GATES * H], BF16, name="w_hh_sb")
         nc.sync.dma_start(w_hh_sb[:], w_hh)
-        h0_sb = held.tile([H, N], BF16, name="h0_sb")
-        nc.scalar.dma_start(h0_sb[:], h0)
+        h0_sb = [held.tile([H, PIECE], BF16, name=f"h0_sb{piece}") for piece in range(PIECES)]
+        nc.scalar.dma_start(h0_sb[0][:], h0[:, 0:PIECE])
 
         table_blocks = table.rearrange("(b p) e -> p b e", p=P)
         rows = []
@@ -45,6 +47,8 @@ def tile_attnseqdecoder_kernel(tc, table, w_ih, w_hh, h0, c0, b_ih, b_hh, offs, 
             queue = nc.sync if chunk % 2 == 0 else nc.scalar
             queue.dma_start(rows[chunk][:], table_blocks[:, chunk * BLOCKS : (chunk + 1) * BLOCKS, :])
 
+        for piece in range(1, PIECES):
+            nc.scalar.dma_start(h0_sb[piece][:], h0[:, piece * PIECE : (piece + 1) * PIECE])
         offsets = held.tile([P, N // 16], U16, name="offsets")
         nc.sync.dma_start(offsets[:], offs)
         w_ih_sb = held.tile([E, GATES * H], BF16, name="w_ih_sb")
@@ -52,10 +56,11 @@ def tile_attnseqdecoder_kernel(tc, table, w_ih, w_hh, h0, c0, b_ih, b_hh, offs, 
         c0_sb = held.tile([H, N], F32, name="c0_sb")
         nc.scalar.dma_start(c0_sb[:], c0)
 
-        nothing = held.tile([P, 1], F32, name="nothing")
-        nc.vector.memset(nothing[:], 0.0)
-        half = held.tile([P, 1], F32, name="half")
-        nc.scalar.activation(half[:], nothing[:], SIGMOID)
+        zeros = held.tile([P, PIECE], BF16, name="zeros")
+        nc.vector.memset(zeros[:], 0.0)
+        unread = psum.tile([P, PIECE], F32, name="unread", tag="bank")
+        for repeat in range(WARM_UP):
+            nc.tensor.matmul(unread[:], zeros[:, 0:P], zeros[:], start=True, stop=True)
 
         small_identity = held.tile([GATES, GATES], F32, name="small_identity")
         masks.make_identity(nc, small_identity[:])
@@ -72,7 +77,7 @@ def tile_attnseqdecoder_kernel(tc, table, w_ih, w_hh, h0, c0, b_ih, b_hh, offs, 
             nc.tensor.matmul(
                 z[gate, piece][:],
                 w_hh_sb[:, gate * H : (gate + 1) * H],
-                h0_sb[:, piece * PIECE : (piece + 1) * PIECE],
+                h0_sb[piece][:],
                 start=True,
                 stop=False,
             )
@@ -96,10 +101,7 @@ def tile_attnseqdecoder_kernel(tc, table, w_ih, w_hh, h0, c0, b_ih, b_hh, offs, 
             flipped = psum.tile([E, CHUNK], BF16, name="flipped", tag="bank")
             for block in range(BLOCKS):
                 nc.tensor.transpose(flipped[:, block * P : (block + 1) * P], rows[chunk][:, block, :], identity[:])
-            if chunk % 2 == 0:
-                nc.vector.tensor_copy(words[:, chunk * CHUNK : (chunk + 1) * CHUNK], flipped[:])
-            else:
-                nc.scalar.copy(words[:, chunk * CHUNK : (chunk + 1) * CHUNK], flipped[:])
+            nc.vector.tensor_copy(words[:, chunk * CHUNK : (chunk + 1) * CHUNK], flipped[:])
 
         for gate in CELL_STATE_GATES:
             hidden_part(gate, 1)
@@ -131,8 +133,9 @@ def tile_attnseqdecoder_kernel(tc, table, w_ih, w_hh, h0, c0, b_ih, b_hh, offs, 
 
         for piece in range(PIECES):
             let_out = gate_value(OUT_GATE, piece, SIGMOID, "let_out")
-            squashed = work.tile([H, PIECE], F32, name="squashed")
-            nc.scalar.activation(squashed[:], cell[piece][:], TANH)
-            hidden = work.tile([H, PIECE], F32, name="hidden")
-            nc.vector.tensor_mul(hidden[:], let_out[:], squashed[:])
-            nc.sync.dma_start(out[:, piece * PIECE : (piece + 1) * PIECE], hidden[:])
+            for start in range(0, PIECE, HALF):
+                squashed = work.tile([H, HALF], F32, name="squashed")
+                nc.scalar.activation(squashed[:], cell[piece][:, start : start + HALF], TANH)
+                hidden = work.tile([H, HALF], F32, name="hidden")
+                nc.vector.tensor_mul(hidden[:], let_out[:, start : start + HALF], squashed[:])
+                nc.sync.dma_start(out[:, piece * PIECE + start : piece * PIECE + start + HALF], hidden[:])

@@ -29,6 +29,7 @@ def tile_attnseqdecoder_kernel(tc, table, w_ih, w_hh, h0, c0, b_ih, b_hh, offs, 
         tc.tile_pool(name="held", bufs=1) as held,
         tc.tile_pool(name="stage", bufs=CHUNKS) as stage,
         tc.tile_pool(name="work", bufs=PIECES) as work,
+        tc.tile_pool(name="results", bufs=N // HALF) as results,
         tc.psum_pool(name="psum", bufs=BANKS) as psum,
     ):
         b_ih_rows = held.tile([GATES, H], F32, name="b_ih_rows")
@@ -136,6 +137,6 @@ def tile_attnseqdecoder_kernel(tc, table, w_ih, w_hh, h0, c0, b_ih, b_hh, offs, 
             for start in range(0, PIECE, HALF):
                 squashed = work.tile([H, HALF], F32, name="squashed")
                 nc.scalar.activation(squashed[:], cell[piece][:, start : start + HALF], TANH)
-                hidden = work.tile([H, HALF], F32, name="hidden")
+                hidden = results.tile([H, HALF], F32, name="hidden")
                 nc.vector.tensor_mul(hidden[:], let_out[:, start : start + HALF], squashed[:])
                 nc.sync.dma_start(out[:, piece * PIECE + start : piece * PIECE + start + HALF], hidden[:])

@@ -41,12 +41,12 @@ def tile_attnseqdecoder_kernel(tc, table, w_ih, w_hh, h0, c0, b_ih, b_hh, offs, 
         h0_sb = [held.tile([H, PIECE], BF16, name=f"h0_sb{piece}") for piece in range(PIECES)]
         nc.scalar.dma_start(h0_sb[0][:], h0[:, 0:PIECE])
 
-        table_blocks = table.rearrange("(b p) e -> p b e", p=P)
+        table_chunks = table.rearrange("(c p t) e -> c p t e", p=P, t=BLOCKS)
         rows = []
         for chunk in range(CHUNKS):
             rows.append(stage.tile([P, BLOCKS, E], BF16, name="rows"))
             queue = nc.sync if chunk % 2 == 0 else nc.scalar
-            queue.dma_start(rows[chunk][:], table_blocks[:, chunk * BLOCKS : (chunk + 1) * BLOCKS, :])
+            queue.dma_start(rows[chunk][:], table_chunks[chunk])
 
         for piece in range(1, PIECES):
             nc.scalar.dma_start(h0_sb[piece][:], h0[:, piece * PIECE : (piece + 1) * PIECE])
@@ -102,7 +102,8 @@ def tile_attnseqdecoder_kernel(tc, table, w_ih, w_hh, h0, c0, b_ih, b_hh, offs, 
             flipped = psum.tile([E, CHUNK], BF16, name="flipped", tag="bank")
             for block in range(BLOCKS):
                 nc.tensor.transpose(flipped[:, block * P : (block + 1) * P], rows[chunk][:, block, :], identity[:])
-            nc.vector.tensor_copy(words[:, chunk * CHUNK : (chunk + 1) * CHUNK], flipped[:])
+            in_order = words[:, chunk * CHUNK : (chunk + 1) * CHUNK].rearrange("e (p t) -> e p t", t=BLOCKS)
+            nc.vector.tensor_copy(in_order, flipped[:].rearrange("e (t p) -> e p t", t=BLOCKS))
 
         for gate in CELL_STATE_GATES:
             hidden_part(gate, 1)

@@ -16,7 +16,6 @@ HALF = PIECE // 2
 CHUNK = 512
 CHUNKS = V // CHUNK
 BLOCKS = CHUNK // P
-WARM_UP = 4
 BANKS = 8
 
 FLOPS = 2 * GATES * H * N * (E + H)
@@ -41,12 +40,12 @@ def tile_attnseqdecoder_kernel(tc, table, w_ih, w_hh, h0, c0, b_ih, b_hh, offs, 
         h0_sb = [held.tile([H, PIECE], BF16, name=f"h0_sb{piece}") for piece in range(PIECES)]
         nc.scalar.dma_start(h0_sb[0][:], h0[:, 0:PIECE])
 
-        table_chunks = table.rearrange("(c p t) e -> c p t e", p=P, t=BLOCKS)
+        table_blocks = table.rearrange("(b p) e -> p b e", p=P)
         rows = []
         for chunk in range(CHUNKS):
             rows.append(stage.tile([P, BLOCKS, E], BF16, name="rows"))
             queue = nc.sync if chunk % 2 == 0 else nc.scalar
-            queue.dma_start(rows[chunk][:], table_chunks[chunk])
+            queue.dma_start(rows[chunk][:], table_blocks[:, chunk * BLOCKS : (chunk + 1) * BLOCKS, :])
 
         for piece in range(1, PIECES):
             nc.scalar.dma_start(h0_sb[piece][:], h0[:, piece * PIECE : (piece + 1) * PIECE])
@@ -56,12 +55,6 @@ def tile_attnseqdecoder_kernel(tc, table, w_ih, w_hh, h0, c0, b_ih, b_hh, offs, 
         nc.sync.dma_start(w_ih_sb[:], w_ih)
         c0_sb = held.tile([H, N], F32, name="c0_sb")
         nc.scalar.dma_start(c0_sb[:], c0)
-
-        zeros = held.tile([P, PIECE], BF16, name="zeros")
-        nc.vector.memset(zeros[:], 0.0)
-        unread = psum.tile([P, PIECE], F32, name="unread", tag="bank")
-        for repeat in range(WARM_UP):
-            nc.tensor.matmul(unread[:], zeros[:, 0:P], zeros[:], start=True, stop=True)
 
         small_identity = held.tile([GATES, GATES], F32, name="small_identity")
         masks.make_identity(nc, small_identity[:])
@@ -102,8 +95,7 @@ def tile_attnseqdecoder_kernel(tc, table, w_ih, w_hh, h0, c0, b_ih, b_hh, offs, 
             flipped = psum.tile([E, CHUNK], BF16, name="flipped", tag="bank")
             for block in range(BLOCKS):
                 nc.tensor.transpose(flipped[:, block * P : (block + 1) * P], rows[chunk][:, block, :], identity[:])
-            in_order = words[:, chunk * CHUNK : (chunk + 1) * CHUNK].rearrange("e (p t) -> e p t", t=BLOCKS)
-            nc.vector.tensor_copy(in_order, flipped[:].rearrange("e (t p) -> e p t", t=BLOCKS))
+            nc.vector.tensor_copy(words[:, chunk * CHUNK : (chunk + 1) * CHUNK], flipped[:])
 
         for gate in CELL_STATE_GATES:
             hidden_part(gate, 1)

@@ -16,6 +16,8 @@ HALF = PIECE // 2
 CHUNK = 512
 CHUNKS = V // CHUNK
 BLOCKS = CHUNK // P
+HALF_TABLE = V // P // 2
+WARM_UP = 3
 BANKS = 8
 
 FLOPS = 2 * GATES * H * N * (E + H)
@@ -26,15 +28,11 @@ def tile_attnseqdecoder_kernel(tc, table, w_ih, w_hh, h0, c0, b_ih, b_hh, offs, 
     nc = tc.nc
     with (
         tc.tile_pool(name="held", bufs=1) as held,
-        tc.tile_pool(name="stage", bufs=CHUNKS) as stage,
+        tc.tile_pool(name="stage", bufs=2) as stage,
         tc.tile_pool(name="work", bufs=PIECES) as work,
         tc.tile_pool(name="results", bufs=N // HALF) as results,
         tc.psum_pool(name="psum", bufs=BANKS) as psum,
     ):
-        b_ih_rows = held.tile([GATES, H], F32, name="b_ih_rows")
-        nc.sync.dma_start(b_ih_rows[:], b_ih.rearrange("(g r) o -> g (r o)", g=GATES))
-        b_hh_rows = held.tile([GATES, H], F32, name="b_hh_rows")
-        nc.sync.dma_start(b_hh_rows[:], b_hh.rearrange("(g r) o -> g (r o)", g=GATES))
         w_hh_sb = held.tile([H, GATES * H], BF16, name="w_hh_sb")
         nc.sync.dma_start(w_hh_sb[:], w_hh)
         h0_sb = [held.tile([H, PIECE], BF16, name=f"h0_sb{piece}") for piece in range(PIECES)]
@@ -42,27 +40,29 @@ def tile_attnseqdecoder_kernel(tc, table, w_ih, w_hh, h0, c0, b_ih, b_hh, offs, 
 
         table_blocks = table.rearrange("(b p) e -> p b e", p=P)
         rows = []
-        for chunk in range(CHUNKS):
-            rows.append(stage.tile([P, BLOCKS, E], BF16, name="rows"))
-            queue = nc.sync if chunk % 2 == 0 else nc.scalar
-            queue.dma_start(rows[chunk][:], table_blocks[:, chunk * BLOCKS : (chunk + 1) * BLOCKS, :])
+        for half, queue in enumerate((nc.sync, nc.scalar)):
+            rows.append(stage.tile([P, HALF_TABLE, E], BF16, name="rows"))
+            queue.dma_start(rows[half][:], table_blocks[:, half * HALF_TABLE : (half + 1) * HALF_TABLE, :])
 
-        for piece in range(1, PIECES):
-            nc.scalar.dma_start(h0_sb[piece][:], h0[:, piece * PIECE : (piece + 1) * PIECE])
-        offsets = held.tile([P, N // 16], U16, name="offsets")
-        nc.sync.dma_start(offsets[:], offs)
         w_ih_sb = held.tile([E, GATES * H], BF16, name="w_ih_sb")
         nc.sync.dma_start(w_ih_sb[:], w_ih)
+        offsets = held.tile([P, N // 16], U16, name="offsets")
+        nc.sync.dma_start(offsets[:], offs)
+        for piece in range(1, PIECES):
+            nc.scalar.dma_start(h0_sb[piece][:], h0[:, piece * PIECE : (piece + 1) * PIECE])
+
+        b_ih_rows = held.tile([GATES, H], F32, name="b_ih_rows")
+        nc.scalar.dma_start(b_ih_rows[:], b_ih.rearrange("(g r) o -> g (r o)", g=GATES))
+        b_hh_rows = held.tile([GATES, H], F32, name="b_hh_rows")
+        nc.scalar.dma_start(b_hh_rows[:], b_hh.rearrange("(g r) o -> g (r o)", g=GATES))
         c0_sb = held.tile([H, N], F32, name="c0_sb")
         nc.scalar.dma_start(c0_sb[:], c0)
 
-        small_identity = held.tile([GATES, GATES], F32, name="small_identity")
-        masks.make_identity(nc, small_identity[:])
-        bias_ps = psum.tile([H, GATES], F32, name="bias_ps", tag="bank")
-        nc.tensor.matmul(bias_ps[:], b_ih_rows[:], small_identity[:], start=True, stop=False)
-        nc.tensor.matmul(bias_ps[:], b_hh_rows[:], small_identity[:], start=False, stop=True)
-        bias = held.tile([H, GATES], F32, name="bias")
-        nc.vector.tensor_copy(bias[:], bias_ps[:])
+        zeros = held.tile([P, PIECE], BF16, name="zeros")
+        nc.vector.memset(zeros[:], 0.0)
+        unread = psum.tile([P, PIECE], F32, name="unread", tag="bank")
+        for repeat in range(WARM_UP):
+            nc.tensor.matmul(unread[:], zeros[:, 0:P], zeros[:], start=True, stop=True)
 
         z = {}
 
@@ -94,8 +94,16 @@ def tile_attnseqdecoder_kernel(tc, table, w_ih, w_hh, h0, c0, b_ih, b_hh, offs, 
         for chunk in range(CHUNKS):
             flipped = psum.tile([E, CHUNK], BF16, name="flipped", tag="bank")
             for block in range(BLOCKS):
-                nc.tensor.transpose(flipped[:, block * P : (block + 1) * P], rows[chunk][:, block, :], identity[:])
+                nc.tensor.transpose(flipped[:, block * P : (block + 1) * P], rows[chunk // 2][:, (chunk % 2) * BLOCKS + block, :], identity[:])
             nc.vector.tensor_copy(words[:, chunk * CHUNK : (chunk + 1) * CHUNK], flipped[:])
+
+        small_identity = held.tile([GATES, GATES], F32, name="small_identity")
+        masks.make_identity(nc, small_identity[:])
+        bias_ps = psum.tile([H, GATES], F32, name="bias_ps", tag="bank")
+        nc.tensor.matmul(bias_ps[:], b_ih_rows[:], small_identity[:], start=True, stop=False)
+        nc.tensor.matmul(bias_ps[:], b_hh_rows[:], small_identity[:], start=False, stop=True)
+        bias = held.tile([H, GATES], F32, name="bias")
+        nc.vector.tensor_copy(bias[:], bias_ps[:])
 
         for gate in CELL_STATE_GATES:
             hidden_part(gate, 1)

@@ -1,9 +1,10 @@
-import concourse.masks as masks
 import concourse.mybir as mybir
+from concourse.masks import make_identity
 
 BF16, F32, U16 = mybir.dt.bfloat16, mybir.dt.float32, mybir.dt.uint16
 SIGMOID = mybir.ActivationFunctionType.Sigmoid
 TANH = mybir.ActivationFunctionType.Tanh
+COPY = mybir.ActivationFunctionType.Copy
 
 P = 128
 V, E, H, N = 2048, 128, 128, 1024
@@ -13,12 +14,11 @@ CELL_STATE_GATES = (FORGET_GATE, IN_GATE, CELL_GATE)
 PIECE = 512
 PIECES = N // PIECE
 HALF = PIECE // 2
+BANKS = 8
 CHUNK = 512
 CHUNKS = V // CHUNK
-BLOCKS = CHUNK // P
-HALF_TABLE = V // P // 2
-WARM_UP = 3
-BANKS = 8
+RUN = CHUNK // P
+WARM_UPS = 2
 
 FLOPS = 2 * GATES * H * N * (E + H)
 BYTES = 2 * N * E + 2 * GATES * H * (E + H) + 2 * H * N + 4 * H * N + 2 * 4 * GATES * H + 2 * P * (N // 16) + 4 * H * N
@@ -28,93 +28,96 @@ def tile_attnseqdecoder_kernel(tc, table, w_ih, w_hh, h0, c0, b_ih, b_hh, offs, 
     nc = tc.nc
     with (
         tc.tile_pool(name="held", bufs=1) as held,
-        tc.tile_pool(name="stage", bufs=2) as stage,
         tc.tile_pool(name="work", bufs=PIECES) as work,
-        tc.tile_pool(name="results", bufs=N // HALF) as results,
+        tc.tile_pool(name="halves", bufs=N // HALF) as halves,
         tc.psum_pool(name="psum", bufs=BANKS) as psum,
     ):
         w_hh_sb = held.tile([H, GATES * H], BF16, name="w_hh_sb")
         nc.sync.dma_start(w_hh_sb[:], w_hh)
         h0_sb = [held.tile([H, PIECE], BF16, name=f"h0_sb{piece}") for piece in range(PIECES)]
         nc.scalar.dma_start(h0_sb[0][:], h0[:, 0:PIECE])
+        rows = [held.tile([P, 2, RUN * E], BF16, name=f"rows{half}") for half in range(2)]
+        in_chunks = table.rearrange("(c p b) e -> p c (b e)", p=P, b=RUN)
+        nc.sync.dma_start(rows[0][:], in_chunks[:, 0:2, :])
+        nc.scalar.dma_start(rows[1][:], in_chunks[:, 2:4, :])
 
-        table_blocks = table.rearrange("(b p) e -> p b e", p=P)
-        rows = []
-        for half, queue in enumerate((nc.sync, nc.scalar)):
-            rows.append(stage.tile([P, HALF_TABLE, E], BF16, name="rows"))
-            queue.dma_start(rows[half][:], table_blocks[:, half * HALF_TABLE : (half + 1) * HALF_TABLE, :])
-
+        nc.scalar.dma_start(h0_sb[1][:], h0[:, PIECE:N])
         w_ih_sb = held.tile([E, GATES * H], BF16, name="w_ih_sb")
         nc.sync.dma_start(w_ih_sb[:], w_ih)
         offsets = held.tile([P, N // 16], U16, name="offsets")
         nc.sync.dma_start(offsets[:], offs)
-        for piece in range(1, PIECES):
-            nc.scalar.dma_start(h0_sb[piece][:], h0[:, piece * PIECE : (piece + 1) * PIECE])
-
-        b_ih_rows = held.tile([GATES, H], F32, name="b_ih_rows")
-        nc.scalar.dma_start(b_ih_rows[:], b_ih.rearrange("(g r) o -> g (r o)", g=GATES))
-        b_hh_rows = held.tile([GATES, H], F32, name="b_hh_rows")
-        nc.scalar.dma_start(b_hh_rows[:], b_hh.rearrange("(g r) o -> g (r o)", g=GATES))
+        b_ih_sb = held.tile([H, GATES], F32, name="b_ih_sb")
+        nc.sync.dma_start(b_ih_sb[:], b_ih.rearrange("(g r) o -> r (g o)", r=H))
+        b_hh_sb = held.tile([H, GATES], F32, name="b_hh_sb")
+        nc.sync.dma_start(b_hh_sb[:], b_hh.rearrange("(g r) o -> r (g o)", r=H))
         c0_sb = held.tile([H, N], F32, name="c0_sb")
-        nc.scalar.dma_start(c0_sb[:], c0)
+        nc.sync.dma_start(c0_sb[:], c0)
+
+        bias = held.tile([H, GATES], F32, name="bias")
+        nc.vector.tensor_add(bias[:], b_ih_sb[:], b_hh_sb[:])
+
+        early = held.tile([P, 1], F32, name="early")
+        nc.vector.memset(early[:], 0.0)
+        nc.scalar.activation(early[:], early[:], SIGMOID)
 
         zeros = held.tile([P, PIECE], BF16, name="zeros")
         nc.vector.memset(zeros[:], 0.0)
         unread = psum.tile([P, PIECE], F32, name="unread", tag="bank")
-        for repeat in range(WARM_UP):
+        for warm_up in range(WARM_UPS):
             nc.tensor.matmul(unread[:], zeros[:, 0:P], zeros[:], start=True, stop=True)
+
+        identity = held.tile([P, P], BF16, name="identity")
+        make_identity(nc, identity[:])
+        words = held.tile([E, V], BF16, name="words")
+
+        def turn(chunk):
+            turned = psum.tile([E, CHUNK], BF16, name="turned", tag="bank")
+            for block in range(RUN):
+                nc.tensor.transpose(turned[:, block * P : (block + 1) * P], rows[chunk // 2][:, chunk % 2, block * E : (block + 1) * E], identity[:])
+            in_order = turned[:].rearrange("e (b p) -> e p b", b=RUN)
+            home = words[:, chunk * CHUNK : (chunk + 1) * CHUNK].rearrange("e (p b) -> e p b", b=RUN)
+            if chunk % 2 == 0:
+                nc.vector.tensor_copy(home, in_order)
+            else:
+                nc.scalar.activation(home, in_order, COPY)
 
         z = {}
 
-        def hidden_part(gate, piece):
-            z[gate, piece] = psum.tile([H, PIECE], F32, name="z", tag="bank")
+        def hidden_part(gate, piece, opens):
             nc.tensor.matmul(
                 z[gate, piece][:],
                 w_hh_sb[:, gate * H : (gate + 1) * H],
                 h0_sb[piece][:],
-                start=True,
-                stop=False,
+                start=opens,
+                stop=not opens,
             )
 
-        def embedding_part(gate, piece):
+        def embedding_part(gate, piece, opens):
             nc.tensor.matmul(
                 z[gate, piece][:],
                 w_ih_sb[:, gate * H : (gate + 1) * H],
                 words[:].indirect(offsets[:, piece * (PIECE // 16) : (piece + 1) * (PIECE // 16)]),
-                start=False,
-                stop=True,
+                start=opens,
+                stop=not opens,
             )
 
-        for gate in CELL_STATE_GATES:
-            hidden_part(gate, 0)
+        early_sums = [(gate, piece) for piece in range(PIECES) for gate in CELL_STATE_GATES] + [(OUT_GATE, 0)]
+        last_sum = (OUT_GATE, 1)
+        def open_sum(gate, piece):
+            z[gate, piece] = psum.tile([H, PIECE], F32, name="z", tag="bank")
+            hidden_part(gate, piece, opens=True)
 
-        identity = held.tile([P, P], BF16, name="identity")
-        masks.make_identity(nc, identity[:])
-        words = held.tile([E, V], BF16, name="words")
+        for gate, piece in early_sums[:3]:
+            open_sum(gate, piece)
         for chunk in range(CHUNKS):
-            flipped = psum.tile([E, CHUNK], BF16, name="flipped", tag="bank")
-            for block in range(BLOCKS):
-                nc.tensor.transpose(flipped[:, block * P : (block + 1) * P], rows[chunk // 2][:, (chunk % 2) * BLOCKS + block, :], identity[:])
-            nc.vector.tensor_copy(words[:, chunk * CHUNK : (chunk + 1) * CHUNK], flipped[:])
-
-        small_identity = held.tile([GATES, GATES], F32, name="small_identity")
-        masks.make_identity(nc, small_identity[:])
-        bias_ps = psum.tile([H, GATES], F32, name="bias_ps", tag="bank")
-        nc.tensor.matmul(bias_ps[:], b_ih_rows[:], small_identity[:], start=True, stop=False)
-        nc.tensor.matmul(bias_ps[:], b_hh_rows[:], small_identity[:], start=False, stop=True)
-        bias = held.tile([H, GATES], F32, name="bias")
-        nc.vector.tensor_copy(bias[:], bias_ps[:])
-
-        for gate in CELL_STATE_GATES:
-            hidden_part(gate, 1)
-        for piece in range(PIECES):
-            hidden_part(OUT_GATE, piece)
-
-        for piece in range(PIECES):
-            for gate in CELL_STATE_GATES:
-                embedding_part(gate, piece)
-        for piece in range(PIECES):
-            embedding_part(OUT_GATE, piece)
+            turn(chunk)
+        for gate, piece in early_sums[3:]:
+            open_sum(gate, piece)
+        z[last_sum] = psum.tile([H, PIECE], F32, name="z", tag="bank")
+        for gate, piece in early_sums:
+            embedding_part(gate, piece, opens=False)
+        embedding_part(*last_sum, opens=True)
+        hidden_part(*last_sum, opens=False)
 
         def gate_value(gate, piece, func, name):
             value = work.tile([H, PIECE], F32, name=name)
@@ -122,22 +125,36 @@ def tile_attnseqdecoder_kernel(tc, table, w_ih, w_hh, h0, c0, b_ih, b_hh, offs, 
             return value
 
         cell = {}
+        starts = range(0, PIECE, HALF)
         for piece in range(PIECES):
             forget = gate_value(FORGET_GATE, piece, SIGMOID, "forget")
             kept = work.tile([H, PIECE], F32, name="kept")
             nc.vector.tensor_mul(kept[:], forget[:], c0_sb[:, piece * PIECE : (piece + 1) * PIECE])
             let_in = gate_value(IN_GATE, piece, SIGMOID, "let_in")
             candidate = gate_value(CELL_GATE, piece, TANH, "candidate")
-            fresh = work.tile([H, PIECE], F32, name="fresh")
-            nc.vector.tensor_mul(fresh[:], let_in[:], candidate[:])
-            cell[piece] = work.tile([H, PIECE], F32, name="cell")
-            nc.vector.tensor_add(cell[piece][:], kept[:], fresh[:])
+            for start in starts:
+                half = slice(start, start + HALF)
+                fresh = halves.tile([H, HALF], F32, name="fresh")
+                nc.vector.tensor_mul(fresh[:], let_in[:, half], candidate[:, half])
+                cell[piece, start] = halves.tile([H, HALF], F32, name="cell")
+                nc.vector.tensor_add(cell[piece, start][:], kept[:, half], fresh[:])
 
+        def squash(piece, start):
+            squashed[piece, start] = halves.tile([H, HALF], F32, name="squashed")
+            nc.scalar.activation(squashed[piece, start][:], cell[piece, start][:], TANH)
+
+        def finish(piece, start):
+            hidden = halves.tile([H, HALF], F32, name="hidden")
+            nc.vector.tensor_mul(hidden[:], let_out[piece][:, start : start + HALF], squashed[piece, start][:])
+            nc.sync.dma_start(out[:, piece * PIECE + start : piece * PIECE + start + HALF], hidden[:])
+
+        squashed, let_out = {}, {}
+        for start in starts:
+            squash(0, start)
         for piece in range(PIECES):
-            let_out = gate_value(OUT_GATE, piece, SIGMOID, "let_out")
-            for start in range(0, PIECE, HALF):
-                squashed = work.tile([H, HALF], F32, name="squashed")
-                nc.scalar.activation(squashed[:], cell[piece][:, start : start + HALF], TANH)
-                hidden = results.tile([H, HALF], F32, name="hidden")
-                nc.vector.tensor_mul(hidden[:], let_out[:, start : start + HALF], squashed[:])
-                nc.sync.dma_start(out[:, piece * PIECE + start : piece * PIECE + start + HALF], hidden[:])
+            let_out[piece] = gate_value(OUT_GATE, piece, SIGMOID, "let_out")
+        for start in starts:
+            finish(0, start)
+        for start in starts:
+            squash(1, start)
+            finish(1, start)

import concourse.mybir as mybir
from concourse.masks import make_identity

BF16, F32, U16 = mybir.dt.bfloat16, mybir.dt.float32, mybir.dt.uint16
SIGMOID = mybir.ActivationFunctionType.Sigmoid
TANH = mybir.ActivationFunctionType.Tanh
COPY = mybir.ActivationFunctionType.Copy

P = 128
V, E, H, N = 2048, 128, 128, 1024
IN_GATE, FORGET_GATE, CELL_GATE, OUT_GATE = 0, 1, 2, 3
GATES = 4
CELL_STATE_GATES = (FORGET_GATE, IN_GATE, CELL_GATE)
PIECE = 512
PIECES = N // PIECE
HALF = PIECE // 2
BANKS = 8
CHUNK = 512
CHUNKS = V // CHUNK
RUN = CHUNK // P
WARM_UPS = 2

FLOPS = 2 * GATES * H * N * (E + H)
BYTES = 2 * N * E + 2 * GATES * H * (E + H) + 2 * H * N + 4 * H * N + 2 * 4 * GATES * H + 2 * P * (N // 16) + 4 * H * N


def tile_attnseqdecoder_kernel(tc, table, w_ih, w_hh, h0, c0, b_ih, b_hh, offs, out):
    nc = tc.nc
    with (
        tc.tile_pool(name="held", bufs=1) as held,
        tc.tile_pool(name="work", bufs=PIECES) as work,
        tc.tile_pool(name="halves", bufs=N // HALF) as halves,
        tc.psum_pool(name="psum", bufs=BANKS) as psum,
    ):
        w_hh_sb = held.tile([H, GATES * H], BF16, name="w_hh_sb")
        nc.sync.dma_start(w_hh_sb[:], w_hh)
        h0_sb = [held.tile([H, PIECE], BF16, name=f"h0_sb{piece}") for piece in range(PIECES)]
        nc.scalar.dma_start(h0_sb[0][:], h0[:, 0:PIECE])
        rows = [held.tile([P, 2, RUN * E], BF16, name=f"rows{half}") for half in range(2)]
        in_chunks = table.rearrange("(c p b) e -> p c (b e)", p=P, b=RUN)
        nc.sync.dma_start(rows[0][:], in_chunks[:, 0:2, :])
        nc.scalar.dma_start(rows[1][:], in_chunks[:, 2:4, :])

        nc.scalar.dma_start(h0_sb[1][:], h0[:, PIECE:N])
        w_ih_sb = held.tile([E, GATES * H], BF16, name="w_ih_sb")
        nc.sync.dma_start(w_ih_sb[:], w_ih)
        offsets = held.tile([P, N // 16], U16, name="offsets")
        nc.sync.dma_start(offsets[:], offs)
        b_ih_sb = held.tile([H, GATES], F32, name="b_ih_sb")
        nc.sync.dma_start(b_ih_sb[:], b_ih.rearrange("(g r) o -> r (g o)", r=H))
        b_hh_sb = held.tile([H, GATES], F32, name="b_hh_sb")
        nc.sync.dma_start(b_hh_sb[:], b_hh.rearrange("(g r) o -> r (g o)", r=H))
        c0_sb = held.tile([H, N], F32, name="c0_sb")
        nc.sync.dma_start(c0_sb[:], c0)

        bias = held.tile([H, GATES], F32, name="bias")
        nc.vector.tensor_add(bias[:], b_ih_sb[:], b_hh_sb[:])

        early = held.tile([P, 1], F32, name="early")
        nc.vector.memset(early[:], 0.0)
        nc.scalar.activation(early[:], early[:], SIGMOID)

        zeros = held.tile([P, PIECE], BF16, name="zeros")
        nc.vector.memset(zeros[:], 0.0)
        unread = psum.tile([P, PIECE], F32, name="unread", tag="bank")
        for warm_up in range(WARM_UPS):
            nc.tensor.matmul(unread[:], zeros[:, 0:P], zeros[:], start=True, stop=True)

        identity = held.tile([P, P], BF16, name="identity")
        make_identity(nc, identity[:])
        words = held.tile([E, V], BF16, name="words")

        def turn(chunk):
            turned = psum.tile([E, CHUNK], BF16, name="turned", tag="bank")
            for block in range(RUN):
                nc.tensor.transpose(turned[:, block * P : (block + 1) * P], rows[chunk // 2][:, chunk % 2, block * E : (block + 1) * E], identity[:])
            in_order = turned[:].rearrange("e (b p) -> e p b", b=RUN)
            home = words[:, chunk * CHUNK : (chunk + 1) * CHUNK].rearrange("e (p b) -> e p b", b=RUN)
            if chunk % 2 == 0:
                nc.vector.tensor_copy(home, in_order)
            else:
                nc.scalar.activation(home, in_order, COPY)

        z = {}

        def hidden_part(gate, piece, opens):
            nc.tensor.matmul(
                z[gate, piece][:],
                w_hh_sb[:, gate * H : (gate + 1) * H],
                h0_sb[piece][:],
                start=opens,
                stop=not opens,
            )

        def embedding_part(gate, piece, opens):
            nc.tensor.matmul(
                z[gate, piece][:],
                w_ih_sb[:, gate * H : (gate + 1) * H],
                words[:].indirect(offsets[:, piece * (PIECE // 16) : (piece + 1) * (PIECE // 16)]),
                start=opens,
                stop=not opens,
            )

        early_sums = [(gate, piece) for piece in range(PIECES) for gate in CELL_STATE_GATES] + [(OUT_GATE, 0)]
        last_sum = (OUT_GATE, 1)
        def open_sum(gate, piece):
            z[gate, piece] = psum.tile([H, PIECE], F32, name="z", tag="bank")
            hidden_part(gate, piece, opens=True)

        for gate, piece in early_sums[:3]:
            open_sum(gate, piece)
        for chunk in range(CHUNKS):
            turn(chunk)
        for gate, piece in early_sums[3:]:
            open_sum(gate, piece)
        z[last_sum] = psum.tile([H, PIECE], F32, name="z", tag="bank")
        for gate, piece in early_sums:
            embedding_part(gate, piece, opens=False)
        embedding_part(*last_sum, opens=True)
        hidden_part(*last_sum, opens=False)

        def gate_value(gate, piece, func, name):
            value = work.tile([H, PIECE], F32, name=name)
            nc.scalar.activation(value[:], z[gate, piece][:], func, bias=bias[:, gate : gate + 1])
            return value

        cell = {}
        starts = range(0, PIECE, HALF)
        for piece in range(PIECES):
            forget = gate_value(FORGET_GATE, piece, SIGMOID, "forget")
            kept = work.tile([H, PIECE], F32, name="kept")
            nc.vector.tensor_mul(kept[:], forget[:], c0_sb[:, piece * PIECE : (piece + 1) * PIECE])
            let_in = gate_value(IN_GATE, piece, SIGMOID, "let_in")
            candidate = gate_value(CELL_GATE, piece, TANH, "candidate")
            for start in starts:
                half = slice(start, start + HALF)
                fresh = halves.tile([H, HALF], F32, name="fresh")
                nc.vector.tensor_mul(fresh[:], let_in[:, half], candidate[:, half])
                cell[piece, start] = halves.tile([H, HALF], F32, name="cell")
                nc.vector.tensor_add(cell[piece, start][:], kept[:, half], fresh[:])

        def squash(piece, start):
            squashed[piece, start] = halves.tile([H, HALF], F32, name="squashed")
            nc.scalar.activation(squashed[piece, start][:], cell[piece, start][:], TANH)

        def finish(piece, start):
            hidden = halves.tile([H, HALF], F32, name="hidden")
            nc.vector.tensor_mul(hidden[:], let_out[piece][:, start : start + HALF], squashed[piece, start][:])
            nc.sync.dma_start(out[:, piece * PIECE + start : piece * PIECE + start + HALF], hidden[:])

        squashed, let_out = {}, {}
        for start in starts:
            squash(0, start)
        for piece in range(PIECES):
            let_out[piece] = gate_value(OUT_GATE, piece, SIGMOID, "let_out")
        for start in starts:
            finish(0, start)
        for start in starts:
            squash(1, start)
            finish(1, start)
